import numpy as np
import ml_dtypes


def mxq(x, axis, fmt="e4m3"):
    dtype, down = {"e4m3": (ml_dtypes.float8_e4m3fn, 7), "e5m2": (ml_dtypes.float8_e5m2, 14)}[fmt]
    v = np.moveaxis(np.asarray(x, np.float32).astype(ml_dtypes.bfloat16).astype(np.float64), axis, -1)
    blocks = v.reshape(v.shape[:-1] + (-1, 32))
    amax = np.abs(blocks).max(-1, keepdims=True)
    byte = np.maximum(np.where(amax > 0, np.frexp(amax)[1] - 1 + 127, 0) - down, 1)
    scale = np.exp2(byte - 127.0)
    codes = (blocks / scale).astype(np.float32).astype(dtype).astype(np.float64)
    return np.moveaxis((codes * scale).reshape(v.shape), -1, axis)


WIDE = False


def mx_kscale(k):
    if not WIDE:
        return np.ones(k)
    levels = np.array([10, -10, 5, -5, 0])
    a = np.random.permutation(np.resize(levels, k // 512 * 4)).reshape(k // 512, 4)
    idx = np.arange(k)
    return np.exp2(a[idx // 512, idx % 128 // 32])


BF16 = ml_dtypes.bfloat16


def bf(x):
    return np.asarray(x, np.float32).astype(BF16)


def f64(x):
    return np.asarray(x).astype(np.float64)


E2M1 = np.array([0.0, 0.5, 1.0, 1.5, 2.0, 3.0, 4.0, 6.0, -0.0, -0.5, -1.0, -1.5, -2.0, -3.0, -4.0, -6.0])


def pack_weight(w, fmt):
    k, n = w.shape
    w = f64(bf(w)).reshape(k // 32, 32, n)
    amax = np.abs(w).max(1)
    if fmt == "e4m3":
        byte = np.frexp(amax)[1] - 1 + 127 - 7
    else:
        mant, ex = np.frexp(amax / 6.0)
        byte = np.where(mant > 0.5, ex, ex - 1) + 127
    byte = np.clip(np.where(amax > 0, byte, 1), 1, 254)
    scaled = (w * np.exp2(127.0 - byte)[:, None, :]).reshape(k, n).astype(np.float32)
    by_word = np.ascontiguousarray(scaled.reshape(k // 512, 128, 4, n).transpose(0, 1, 3, 2))
    if fmt == "e4m3":
        words = by_word.astype(ml_dtypes.float8_e4m3fn).view(np.uint8)
    else:
        c = by_word.astype(ml_dtypes.float4_e2m1fn).view(np.uint8) & 0xF
        words = c[..., 0::2] | (c[..., 1::2] << 4)
    return np.ascontiguousarray(words), np.ascontiguousarray(byte.astype(np.uint8).reshape(k // 512, 16, n))


def unpack_weight(words, scales, fmt):
    g, p, n, _ = words.shape
    if fmt == "e4m3":
        vals = np.ascontiguousarray(words).view(ml_dtypes.float8_e4m3fn).astype(np.float64)
    else:
        nib = np.empty((g, p, n, 4), np.uint8)
        nib[..., 0::2] = words & 0xF
        nib[..., 1::2] = words >> 4
        vals = E2M1[nib]
    vals = vals * np.repeat(np.exp2(scales.astype(np.float64) - 127.0), 8, axis=1)[..., None]
    return vals.transpose(0, 1, 3, 2).reshape(g * 512, n)


B, S, D_IN, D_OUT = 2, 256, 2048, 2048


def quant8(w):
    mv = np.max(np.abs(w))
    q = np.ceil(np.log2(mv)) - 6.0
    scale = np.exp2(q)
    return np.round(w / scale) * scale


def setup_inputs():
    s = mx_kscale(D_IN)
    x = np.random.standard_normal((B, S, D_IN))
    weight = np.random.standard_normal((D_OUT, D_IN)) * 3.0 / np.sqrt(D_IN)
    w_upper = quant8(weight)
    w_lower = weight - w_upper
    upper_words, upper_scales = pack_weight((w_upper / s[None, :]).T, "e4m3")
    lower_words, lower_scales = pack_weight((w_lower / s[None, :]).T, "e4m3")
    return {"x": bf(x * s), "weight_upper_words": upper_words, "weight_upper_scales": upper_scales, "weight_lower_words": lower_words, "weight_lower_scales": lower_scales}


def reference(x, weight_upper_words, weight_upper_scales, weight_lower_words, weight_lower_scales):
    xq = mxq(f64(x), 2, "e4m3")
    y_upper = xq @ unpack_weight(weight_upper_words, weight_upper_scales, "e4m3")
    y_lower = xq @ unpack_weight(weight_lower_words, weight_lower_scales, "e4m3")
    return y_upper + y_lower

@@ -1,0 +1,146 @@
+from contextlib import ExitStack
+
+import concourse.mybir as mybir
+from concourse.masks import make_identity
+
+F32 = mybir.dt.float32
+BF16 = mybir.dt.bfloat16
+I32 = mybir.dt.int32
+U32 = mybir.dt.uint32
+U8 = mybir.dt.uint8
+FP8X4 = mybir.dt.float8_e4m3fn_x4
+
+P = 128
+PACK = 4
+K_PASS = P * PACK
+TOKENS = 512
+D_IN = 2048
+D_OUT = 2048
+PASSES = D_IN // K_PASS
+TOKEN_TILES = TOKENS // P
+N_COLS = 512
+N_CHUNKS = D_OUT // N_COLS
+WORDS_PER_PASS = K_PASS // 2
+PASSES_PER_BANK = 2
+QUADRANTS = 4
+PLANE_ROWS = 4
+PSUM_BANKS = 8
+
+FLOPS = 2 * 2 * TOKENS * D_IN * D_OUT
+
+
+def load_scale_planes(nc, planes, scales):
+    rows = PASSES * PLANE_ROWS
+    for quadrant in range(QUADRANTS):
+        nc.sync.dma_start(
+            out=planes[32 * quadrant : 32 * quadrant + rows, :].bitcast(I32),
+            in_=scales[:, PLANE_ROWS * quadrant : PLANE_ROWS * (quadrant + 1), :].bitcast(I32),
+        )
+
+
+def load_words(nc, words_sb, words, g, cols):
+    nc.sync.dma_start(
+        out=words_sb[:, g, cols].bitcast(I32),
+        in_=words[g, :, cols, :].rearrange("p n t -> p (n t)").bitcast(I32),
+    )
+
+
+def tile_virtual16bmatmul_kernel(
+    tc,
+    x,
+    weight_upper_words,
+    weight_upper_scales,
+    weight_lower_words,
+    weight_lower_scales,
+    out,
+):
+    nc = tc.nc
+    x_rows = x.flatten_outer_dims()
+    out_rows = out.flatten_outer_dims()
+    dram_words = (weight_upper_words, weight_lower_words)
+    dram_scales = (weight_upper_scales, weight_lower_scales)
+    n_weights = len(dram_words)
+    chunk_cols = [slice(N_COLS * j, N_COLS * (j + 1)) for j in range(N_CHUNKS)]
+
+    with ExitStack() as ctx:
+        ctx.enter_context(tc.manual_schedule())
+        keep = ctx.enter_context(tc.tile_pool(name="keep", bufs=1))
+        stage = ctx.enter_context(tc.tile_pool(name="stage", bufs=4))
+        results = ctx.enter_context(tc.tile_pool(name="results", bufs=8))
+        psum = ctx.enter_context(tc.psum_pool(name="psum", bufs=PSUM_BANKS))
+
+        identity = keep.tile([P, P], F32, name="identity")
+        make_identity(nc, identity[:])
+
+        x_raw = keep.tile([P, TOKEN_TILES, D_IN], BF16, name="x_raw")
+        x_codes = keep.tile([P, TOKEN_TILES, PASSES, P], U32, name="x_codes", align_bytes=64)
+        x_scales = keep.tile([P, TOKEN_TILES, PASSES, P], U8, name="x_scales", align_bytes=64)
+        w_words = [
+            keep.tile([P, PASSES, D_OUT], U32, name="w_words_%d" % w, align_bytes=64)
+            for w in range(n_weights)
+        ]
+        w_planes = [
+            keep.tile([P, D_OUT], U8, name="w_planes_%d" % w, align_bytes=64)
+            for w in range(n_weights)
+        ]
+
+        for w in range(n_weights):
+            nc.vector.memset(w_planes[w][:].bitcast(I32), 0)
+
+        for m in range(TOKEN_TILES):
+            nc.sync.dma_start(out=x_raw[:, m, :], in_=x_rows[P * m : P * (m + 1), :])
+        for j in range(N_CHUNKS):
+            for w in range(n_weights):
+                if j == 0:
+                    load_scale_planes(nc, w_planes[w], dram_scales[w])
+                for g in range(PASSES):
+                    load_words(nc, w_words[w], dram_words[w], g, chunk_cols[j])
+
+        for m in range(TOKEN_TILES):
+            x_words = x_raw[:, m, :].bitcast(F32)
+            for first_pass in range(0, PASSES, PASSES_PER_BANK):
+                flipped = psum.tile([P, PASSES_PER_BANK, 2, P], F32, name="flipped", tag="bank")
+                for i in range(PASSES_PER_BANK):
+                    first_word = WORDS_PER_PASS * (first_pass + i)
+                    for u in range(2):
+                        nc.tensor.transpose(
+                            flipped[:, i, u, :],
+                            x_words[:, first_word + u : first_word + WORDS_PER_PASS : 2],
+                            identity[:],
+                        )
+                grouped = stage.tile([P, PASSES_PER_BANK, P, PACK], BF16, name="grouped", align_bytes=64)
+                nc.scalar.copy(
+                    out=grouped[:].bitcast(F32),
+                    in_=flipped[:].rearrange("p i u r -> p i r u"),
+                )
+                these = slice(first_pass, first_pass + PASSES_PER_BANK)
+                nc.vector.quantize_mx(
+                    out=x_codes[:, m, these, :].rearrange("p i r -> p (i r)").bitcast(FP8X4),
+                    scales=x_scales[:, m, these, :].rearrange("p i r -> p (i r)"),
+                    in_=grouped[:].rearrange("p i r t -> p (i r t)"),
+                )
+
+        for j in range(N_CHUNKS):
+            acc = [
+                psum.tile([P, N_COLS], F32, name="acc_%d" % m, tag="bank")
+                for m in range(TOKEN_TILES)
+            ]
+            for w in range(n_weights):
+                for g in range(PASSES):
+                    for m in range(TOKEN_TILES):
+                        nc.tensor.matmul_mx(
+                            out=acc[m][:],
+                            lhsT=x_codes[:, m, g, :].bitcast(FP8X4),
+                            lhsT_scale=x_scales[:, m, g, :],
+                            rhs=w_words[w][:, g, chunk_cols[j]].bitcast(FP8X4),
+                            rhs_scale=w_planes[w][PLANE_ROWS * g : P, chunk_cols[j]],
+                            start=(w == 0 and g == 0),
+                            stop=(w == n_weights - 1 and g == PASSES - 1),
+                        )
+            for m in range(TOKEN_TILES):
+                result = results.tile([P, N_COLS], F32, name="result")
+                if m % 2 == 0:
+                    nc.vector.tensor_copy(out=result[:], in_=acc[m][:])
+                else:
+                    nc.scalar.copy(out=result[:], in_=acc[m][:])
+                nc.sync.dma_start(out=out_rows[P * m : P * (m + 1), chunk_cols[j]], in_=result[:])

@@ -29,12 +29,12 @@ PSUM_BANKS = 8
 FLOPS = 2 * 2 * TOKENS * D_IN * D_OUT
 
 
-def load_scale_planes(nc, planes, scales):
+def load_scale_planes(nc, planes, scales, cols):
     rows = PASSES * PLANE_ROWS
     for quadrant in range(QUADRANTS):
         nc.sync.dma_start(
-            out=planes[32 * quadrant : 32 * quadrant + rows, :].bitcast(I32),
-            in_=scales[:, PLANE_ROWS * quadrant : PLANE_ROWS * (quadrant + 1), :].bitcast(I32),
+            out=planes[32 * quadrant : 32 * quadrant + rows, cols].bitcast(I32),
+            in_=scales[:, PLANE_ROWS * quadrant : PLANE_ROWS * (quadrant + 1), cols].bitcast(I32),
         )
 
 
@@ -91,8 +91,7 @@ def tile_virtual16bmatmul_kernel(
             nc.sync.dma_start(out=x_raw[:, m, :], in_=x_rows[P * m : P * (m + 1), :])
         for j in range(N_CHUNKS):
             for w in range(n_weights):
-                if j == 0:
-                    load_scale_planes(nc, w_planes[w], dram_scales[w])
+                load_scale_planes(nc, w_planes[w], dram_scales[w], chunk_cols[j])
                 for g in range(PASSES):
                     load_words(nc, w_words[w], dram_words[w], g, chunk_cols[j])
 
@@ -125,18 +124,21 @@ def tile_virtual16bmatmul_kernel(
                 psum.tile([P, N_COLS], F32, name="acc_%d" % m, tag="bank")
                 for m in range(TOKEN_TILES)
             ]
-            for w in range(n_weights):
-                for g in range(PASSES):
-                    for m in range(TOKEN_TILES):
-                        nc.tensor.matmul_mx(
-                            out=acc[m][:],
-                            lhsT=x_codes[:, m, g, :].bitcast(FP8X4),
-                            lhsT_scale=x_scales[:, m, g, :],
-                            rhs=w_words[w][:, g, chunk_cols[j]].bitcast(FP8X4),
-                            rhs_scale=w_planes[w][PLANE_ROWS * g : P, chunk_cols[j]],
-                            start=(w == 0 and g == 0),
-                            stop=(w == n_weights - 1 and g == PASSES - 1),
-                        )
+            pieces = [(w, g) for w in range(n_weights) for g in range(PASSES)]
+            if j < N_CHUNKS - 1:
+                order = [(w, g, m) for (w, g) in pieces for m in range(TOKEN_TILES)]
+            else:
+                order = [(w, g, m) for m in range(TOKEN_TILES) for (w, g) in pieces]
+            for w, g, m in order:
+                nc.tensor.matmul_mx(
+                    out=acc[m][:],
+                    lhsT=x_codes[:, m, g, :].bitcast(FP8X4),
+                    lhsT_scale=x_scales[:, m, g, :],
+                    rhs=w_words[w][:, g, chunk_cols[j]].bitcast(FP8X4),
+                    rhs_scale=w_planes[w][PLANE_ROWS * g : P, chunk_cols[j]],
+                    start=((w, g) == pieces[0]),
+                    stop=((w, g) == pieces[-1]),
+                )
             for m in range(TOKEN_TILES):
                 result = results.tile([P, N_COLS], F32, name="result")
                 if m % 2 == 0:

@@ -21,7 +21,7 @@ TOKEN_TILES = TOKENS // P
 N_COLS = 512
 N_CHUNKS = D_OUT // N_COLS
 WORDS_PER_PASS = K_PASS // 2
-PASSES_PER_BANK = 2
+TILES_PER_BANK = 2
 QUADRANTS = 4
 PLANE_ROWS = 4
 PSUM_BANKS = 8
@@ -57,6 +57,7 @@ def tile_virtual16bmatmul_kernel(
     nc = tc.nc
     x_rows = x.flatten_outer_dims()
     out_rows = out.flatten_outer_dims()
+    x_by_tile = x_rows.rearrange("(m p) k -> p m k", p=P)
     dram_words = (weight_upper_words, weight_lower_words)
     dram_scales = (weight_upper_scales, weight_lower_scales)
     n_weights = len(dram_words)
@@ -67,14 +68,20 @@ def tile_virtual16bmatmul_kernel(
         keep = ctx.enter_context(tc.tile_pool(name="keep", bufs=1))
         stage = ctx.enter_context(tc.tile_pool(name="stage", bufs=4))
         results = ctx.enter_context(tc.tile_pool(name="results", bufs=8))
-        psum = ctx.enter_context(tc.psum_pool(name="psum", bufs=PSUM_BANKS))
+        psum = ctx.enter_context(tc.psum_pool(name="psum", bufs=1))
 
         identity = keep.tile([P, P], F32, name="identity")
         make_identity(nc, identity[:])
 
-        x_raw = keep.tile([P, TOKEN_TILES, D_IN], BF16, name="x_raw")
-        x_codes = keep.tile([P, TOKEN_TILES, PASSES, P], U32, name="x_codes", align_bytes=64)
-        x_scales = keep.tile([P, TOKEN_TILES, PASSES, P], U8, name="x_scales", align_bytes=64)
+        x_raw = [keep.tile([P, TOKEN_TILES, K_PASS], BF16, name="x_raw_%d" % g) for g in range(PASSES)]
+        x_codes = [
+            keep.tile([P, TOKEN_TILES, P], U32, name="x_codes_%d" % g, align_bytes=64)
+            for g in range(PASSES)
+        ]
+        x_scales = [
+            keep.tile([P, TOKEN_TILES, P], U8, name="x_scales_%d" % g, align_bytes=64)
+            for g in range(PASSES)
+        ]
         w_words = [
             keep.tile([P, PASSES, D_OUT], U32, name="w_words_%d" % w, align_bytes=64)
             for w in range(n_weights)
@@ -84,61 +91,90 @@ def tile_virtual16bmatmul_kernel(
             for w in range(n_weights)
         ]
 
-        for w in range(n_weights):
-            nc.vector.memset(w_planes[w][:].bitcast(I32), 0)
-
-        for m in range(TOKEN_TILES):
-            nc.sync.dma_start(out=x_raw[:, m, :], in_=x_rows[P * m : P * (m + 1), :])
         for j in range(N_CHUNKS):
+            for w in range(n_weights):
+                nc.vector.memset(w_planes[w][:, chunk_cols[j]].bitcast(I32), 0)
+
+        def load_x(g, first_tile, n_tiles):
+            tiles = slice(first_tile, first_tile + n_tiles)
+            nc.sync.dma_start(
+                out=x_raw[g][:, tiles, :],
+                in_=x_by_tile[:, tiles, K_PASS * g : K_PASS * (g + 1)],
+            )
+
+        load_x(0, 0, TILES_PER_BANK)
+        load_scale_planes(nc, w_planes[0], dram_scales[0], chunk_cols[0])
+        load_x(0, TILES_PER_BANK, TILES_PER_BANK)
+        load_x(1, 0, TILES_PER_BANK)
+        load_x(1, TILES_PER_BANK, TILES_PER_BANK)
+        load_words(nc, w_words[0], dram_words[0], 0, chunk_cols[0])
+        load_scale_planes(nc, w_planes[1], dram_scales[1], chunk_cols[0])
+        load_words(nc, w_words[1], dram_words[1], 0, chunk_cols[0])
+        for g in range(1, PASSES):
+            if g + 1 < PASSES:
+                load_x(g + 1, 0, TOKEN_TILES)
+            for w in range(n_weights):
+                load_words(nc, w_words[w], dram_words[w], g, chunk_cols[0])
+        for j in range(1, N_CHUNKS):
             for w in range(n_weights):
                 load_scale_planes(nc, w_planes[w], dram_scales[w], chunk_cols[j])
                 for g in range(PASSES):
                     load_words(nc, w_words[w], dram_words[w], g, chunk_cols[j])
 
-        for m in range(TOKEN_TILES):
-            x_words = x_raw[:, m, :].bitcast(F32)
-            for first_pass in range(0, PASSES, PASSES_PER_BANK):
-                flipped = psum.tile([P, PASSES_PER_BANK, 2, P], F32, name="flipped", tag="bank")
-                for i in range(PASSES_PER_BANK):
-                    first_word = WORDS_PER_PASS * (first_pass + i)
+        def quantise_x(g, banks):
+            for half, bank in enumerate(banks):
+                first_tile = TILES_PER_BANK * half
+                flipped = psum.tile([P, TILES_PER_BANK, 2, P], F32, name="flipped", tag="bank%d" % bank)
+                for i in range(TILES_PER_BANK):
+                    x_words = x_raw[g][:, first_tile + i, :].bitcast(F32)
                     for u in range(2):
-                        nc.tensor.transpose(
-                            flipped[:, i, u, :],
-                            x_words[:, first_word + u : first_word + WORDS_PER_PASS : 2],
-                            identity[:],
-                        )
-                grouped = stage.tile([P, PASSES_PER_BANK, P, PACK], BF16, name="grouped", align_bytes=64)
+                        nc.tensor.transpose(flipped[:, i, u, :], x_words[:, u:WORDS_PER_PASS:2], identity[:])
+                grouped = stage.tile([P, TILES_PER_BANK, P, PACK], BF16, name="grouped", align_bytes=64)
                 nc.scalar.copy(
                     out=grouped[:].bitcast(F32),
                     in_=flipped[:].rearrange("p i u r -> p i r u"),
                 )
-                these = slice(first_pass, first_pass + PASSES_PER_BANK)
+                these = slice(first_tile, first_tile + TILES_PER_BANK)
                 nc.vector.quantize_mx(
-                    out=x_codes[:, m, these, :].rearrange("p i r -> p (i r)").bitcast(FP8X4),
-                    scales=x_scales[:, m, these, :].rearrange("p i r -> p (i r)"),
+                    out=x_codes[g][:, these, :].rearrange("p i r -> p (i r)").bitcast(FP8X4),
+                    scales=x_scales[g][:, these, :].rearrange("p i r -> p (i r)"),
                     in_=grouped[:].rearrange("p i r t -> p (i r t)"),
                 )
 
+        def multiply(acc, j, w, g, m, first, last):
+            nc.tensor.matmul_mx(
+                out=acc[m][:],
+                lhsT=x_codes[g][:, m, :].bitcast(FP8X4),
+                lhsT_scale=x_scales[g][:, m, :],
+                rhs=w_words[w][:, g, chunk_cols[j]].bitcast(FP8X4),
+                rhs_scale=w_planes[w][PLANE_ROWS * g : P, chunk_cols[j]],
+                start=first,
+                stop=last,
+            )
+
         for j in range(N_CHUNKS):
+            first_bank = TOKEN_TILES * (j % 2)
             acc = [
-                psum.tile([P, N_COLS], F32, name="acc_%d" % m, tag="bank")
+                psum.tile([P, N_COLS], F32, name="acc_%d" % m, tag="bank%d" % (first_bank + m))
                 for m in range(TOKEN_TILES)
             ]
-            pieces = [(w, g) for w in range(n_weights) for g in range(PASSES)]
-            if j < N_CHUNKS - 1:
-                order = [(w, g, m) for (w, g) in pieces for m in range(TOKEN_TILES)]
+            if j == 0:
+                pieces = [(w, g) for g in range(PASSES) for w in range(n_weights)]
+                quantise_x(0, (4, 5))
+                quantise_x(1, (6, 7))
+                for w, g in pieces:
+                    for m in range(TOKEN_TILES):
+                        multiply(acc, j, w, g, m, (w, g) == pieces[0], (w, g) == pieces[-1])
+                    if w == n_weights - 1 and g + 2 < PASSES:
+                        quantise_x(g + 2, (4, 5) if g % 2 == 0 else (6, 7))
             else:
-                order = [(w, g, m) for m in range(TOKEN_TILES) for (w, g) in pieces]
-            for w, g, m in order:
-                nc.tensor.matmul_mx(
-                    out=acc[m][:],
-                    lhsT=x_codes[:, m, g, :].bitcast(FP8X4),
-                    lhsT_scale=x_scales[:, m, g, :],
-                    rhs=w_words[w][:, g, chunk_cols[j]].bitcast(FP8X4),
-                    rhs_scale=w_planes[w][PLANE_ROWS * g : P, chunk_cols[j]],
-                    start=((w, g) == pieces[0]),
-                    stop=((w, g) == pieces[-1]),
-                )
+                pieces = [(w, g) for w in range(n_weights) for g in range(PASSES)]
+                if j < N_CHUNKS - 1:
+                    order = [(w, g, m) for (w, g) in pieces for m in range(TOKEN_TILES)]
+                else:
+                    order = [(w, g, m) for m in range(TOKEN_TILES) for (w, g) in pieces]
+                for w, g, m in order:
+                    multiply(acc, j, w, g, m, (w, g) == pieces[0], (w, g) == pieces[-1])
             for m in range(TOKEN_TILES):
                 result = results.tile([P, N_COLS], F32, name="result")
                 if m % 2 == 0:

@@ -25,6 +25,7 @@ TILES_PER_BANK = 2
 QUADRANTS = 4
 PLANE_ROWS = 4
 PSUM_BANKS = 8
+WARM_UP = 5
 
 FLOPS = 2 * 2 * TOKENS * D_IN * D_OUT
 
@@ -72,6 +73,14 @@ def tile_virtual16bmatmul_kernel(
 
         identity = keep.tile([P, P], F32, name="identity")
         make_identity(nc, identity[:])
+
+        zeros = keep.tile([P, N_COLS], BF16, name="zeros")
+        nc.vector.memset(zeros[:], 0.0)
+        unread = psum.tile([P, N_COLS], F32, name="unread", tag="bank0")
+
+        def keep_busy(n_matmuls):
+            for i in range(n_matmuls):
+                nc.tensor.matmul(unread[:], lhsT=zeros[:, 0:P], rhs=zeros[:], start=True, stop=True)
 
         x_raw = [keep.tile([P, TOKEN_TILES, K_PASS], BF16, name="x_raw_%d" % g) for g in range(PASSES)]
         x_codes = [
@@ -121,7 +130,7 @@ def tile_virtual16bmatmul_kernel(
                 for g in range(PASSES):
                     load_words(nc, w_words[w], dram_words[w], g, chunk_cols[j])
 
-        def quantise_x(g, banks):
+        def quantise_x(g, banks, dummies=0):
             for half, bank in enumerate(banks):
                 first_tile = TILES_PER_BANK * half
                 flipped = psum.tile([P, TILES_PER_BANK, 2, P], F32, name="flipped", tag="bank%d" % bank)
@@ -129,6 +138,7 @@ def tile_virtual16bmatmul_kernel(
                     x_words = x_raw[g][:, first_tile + i, :].bitcast(F32)
                     for u in range(2):
                         nc.tensor.transpose(flipped[:, i, u, :], x_words[:, u:WORDS_PER_PASS:2], identity[:])
+                keep_busy(dummies)
                 grouped = stage.tile([P, TILES_PER_BANK, P, PACK], BF16, name="grouped", align_bytes=64)
                 nc.scalar.copy(
                     out=grouped[:].bitcast(F32),
@@ -152,6 +162,10 @@ def tile_virtual16bmatmul_kernel(
                 stop=last,
             )
 
+        keep_busy(WARM_UP)
+        quantise_x(0, (4, 5), dummies=1)
+        quantise_x(1, (6, 7), dummies=1)
+
         for j in range(N_CHUNKS):
             first_bank = TOKEN_TILES * (j % 2)
             acc = [
@@ -160,8 +174,6 @@ def tile_virtual16bmatmul_kernel(
             ]
             if j == 0:
                 pieces = [(w, g) for g in range(PASSES) for w in range(n_weights)]
-                quantise_x(0, (4, 5))
-                quantise_x(1, (6, 7))
                 for w, g in pieces:
                     for m in range(TOKEN_TILES):
                         multiply(acc, j, w, g, m, (w, g) == pieces[0], (w, g) == pieces[-1])

@@ -25,6 +25,7 @@ TILES_PER_BANK = 2
 QUADRANTS = 4
 PLANE_ROWS = 4
 PSUM_BANKS = 8
+LAST_WIDTHS = (256, 128, 128)
 WARM_UP = 5
 
 FLOPS = 2 * 2 * TOKENS * D_IN * D_OUT
@@ -151,22 +152,31 @@ def tile_virtual16bmatmul_kernel(
                     in_=grouped[:].rearrange("p i r t -> p (i r t)"),
                 )
 
-        def multiply(acc, j, w, g, m, first, last):
+        def multiply(group, cols, w, g, m, first, last):
             nc.tensor.matmul_mx(
-                out=acc[m][:],
+                out=group,
                 lhsT=x_codes[g][:, m, :].bitcast(FP8X4),
                 lhsT_scale=x_scales[g][:, m, :],
-                rhs=w_words[w][:, g, chunk_cols[j]].bitcast(FP8X4),
-                rhs_scale=w_planes[w][PLANE_ROWS * g : P, chunk_cols[j]],
+                rhs=w_words[w][:, g, cols].bitcast(FP8X4),
+                rhs_scale=w_planes[w][PLANE_ROWS * g : P, cols],
                 start=first,
                 stop=last,
             )
+
+        def leave(group, cols, m, turn):
+            width = cols.stop - cols.start
+            result = results.tile([P, N_COLS], F32, name="result")
+            if turn % 2 == 0:
+                nc.vector.tensor_copy(out=result[:, 0:width], in_=group)
+            else:
+                nc.scalar.copy(out=result[:, 0:width], in_=group)
+            nc.sync.dma_start(out=out_rows[P * m : P * (m + 1), cols], in_=result[:, 0:width])
 
         keep_busy(WARM_UP)
         quantise_x(0, (4, 5), dummies=1)
         quantise_x(1, (6, 7), dummies=1)
 
-        for j in range(N_CHUNKS):
+        for j in range(N_CHUNKS - 1):
             first_bank = TOKEN_TILES * (j % 2)
             acc = [
                 psum.tile([P, N_COLS], F32, name="acc_%d" % m, tag="bank%d" % (first_bank + m))
@@ -174,23 +184,26 @@ def tile_virtual16bmatmul_kernel(
             ]
             if j == 0:
                 pieces = [(w, g) for g in range(PASSES) for w in range(n_weights)]
-                for w, g in pieces:
-                    for m in range(TOKEN_TILES):
-                        multiply(acc, j, w, g, m, (w, g) == pieces[0], (w, g) == pieces[-1])
-                    if w == n_weights - 1 and g + 2 < PASSES:
-                        quantise_x(g + 2, (4, 5) if g % 2 == 0 else (6, 7))
             else:
                 pieces = [(w, g) for w in range(n_weights) for g in range(PASSES)]
-                if j < N_CHUNKS - 1:
-                    order = [(w, g, m) for (w, g) in pieces for m in range(TOKEN_TILES)]
-                else:
-                    order = [(w, g, m) for m in range(TOKEN_TILES) for (w, g) in pieces]
-                for w, g, m in order:
-                    multiply(acc, j, w, g, m, (w, g) == pieces[0], (w, g) == pieces[-1])
+            for w, g in pieces:
+                for m in range(TOKEN_TILES):
+                    multiply(acc[m][:], chunk_cols[j], w, g, m, (w, g) == pieces[0], (w, g) == pieces[-1])
+                if j == 0 and w == n_weights - 1 and g + 2 < PASSES:
+                    quantise_x(g + 2, (4, 5) if g % 2 == 0 else (6, 7))
             for m in range(TOKEN_TILES):
-                result = results.tile([P, N_COLS], F32, name="result")
-                if m % 2 == 0:
-                    nc.vector.tensor_copy(out=result[:], in_=acc[m][:])
-                else:
-                    nc.scalar.copy(out=result[:], in_=acc[m][:])
-                nc.sync.dma_start(out=out_rows[P * m : P * (m + 1), chunk_cols[j]], in_=result[:])
+                leave(acc[m][:], chunk_cols[j], m, m)
+
+        first_col = N_COLS * (N_CHUNKS - 1)
+        groups = [(m, first_col, N_COLS) for m in range(TOKEN_TILES - 1)]
+        for width in LAST_WIDTHS:
+            groups.append((TOKEN_TILES - 1, first_col, width))
+            first_col += width
+        pieces = [(w, g) for w in range(n_weights) for g in range(PASSES)]
+        for turn, (m, col, width) in enumerate(groups):
+            bank = (TOKEN_TILES + turn) % PSUM_BANKS
+            acc_last = psum.tile([P, N_COLS], F32, name="acc_last", tag="bank%d" % bank)
+            cols = slice(col, col + width)
+            for w, g in pieces:
+                multiply(acc_last[:, 0:width], cols, w, g, m, (w, g) == pieces[0], (w, g) == pieces[-1])
+            leave(acc_last[:, 0:width], cols, m, turn)

@@ -131,26 +131,36 @@ def tile_virtual16bmatmul_kernel(
                 for g in range(PASSES):
                     load_words(nc, w_words[w], dram_words[w], g, chunk_cols[j])
 
-        def quantise_x(g, banks, dummies=0):
-            for half, bank in enumerate(banks):
-                first_tile = TILES_PER_BANK * half
-                flipped = psum.tile([P, TILES_PER_BANK, 2, P], F32, name="flipped", tag="bank%d" % bank)
-                for i in range(TILES_PER_BANK):
-                    x_words = x_raw[g][:, first_tile + i, :].bitcast(F32)
-                    for u in range(2):
-                        nc.tensor.transpose(flipped[:, i, u, :], x_words[:, u:WORDS_PER_PASS:2], identity[:])
-                keep_busy(dummies)
-                grouped = stage.tile([P, TILES_PER_BANK, P, PACK], BF16, name="grouped", align_bytes=64)
-                nc.scalar.copy(
-                    out=grouped[:].bitcast(F32),
-                    in_=flipped[:].rearrange("p i u r -> p i r u"),
-                )
-                these = slice(first_tile, first_tile + TILES_PER_BANK)
-                nc.vector.quantize_mx(
-                    out=x_codes[g][:, these, :].rearrange("p i r -> p (i r)").bitcast(FP8X4),
-                    scales=x_scales[g][:, these, :].rearrange("p i r -> p (i r)"),
-                    in_=grouped[:].rearrange("p i r t -> p (i r t)"),
-                )
+        def tiles_of(half):
+            return slice(TILES_PER_BANK * half, TILES_PER_BANK * (half + 1))
+
+        def split_words(g, half):
+            x_split = stage.tile([P, TILES_PER_BANK, 2, P], F32, name="x_split")
+            nc.vector.tensor_copy(
+                out=x_split[:],
+                in_=x_raw[g][:, tiles_of(half), :].bitcast(F32).rearrange("p i (r u) -> p i u r", u=2),
+            )
+            return x_split
+
+        def flip(x_split, bank, dummies=0):
+            flipped = psum.tile([P, TILES_PER_BANK, 2, P], F32, name="flipped", tag="bank%d" % bank)
+            for i in range(TILES_PER_BANK):
+                for u in range(2):
+                    nc.tensor.transpose(flipped[:, i, u, :], x_split[:, i, u, :], identity[:])
+            keep_busy(dummies)
+            grouped = stage.tile([P, TILES_PER_BANK, P, PACK], BF16, name="grouped", align_bytes=64)
+            nc.scalar.copy(
+                out=grouped[:].bitcast(F32),
+                in_=flipped[:].rearrange("p i u r -> p i r u"),
+            )
+            return grouped
+
+        def quantise(grouped, g, half):
+            nc.vector.quantize_mx(
+                out=x_codes[g][:, tiles_of(half), :].rearrange("p i r -> p (i r)").bitcast(FP8X4),
+                scales=x_scales[g][:, tiles_of(half), :].rearrange("p i r -> p (i r)"),
+                in_=grouped[:].rearrange("p i r t -> p (i r t)"),
+            )
 
         def multiply(group, cols, w, g, m, first, last):
             nc.tensor.matmul_mx(
@@ -173,8 +183,14 @@ def tile_virtual16bmatmul_kernel(
             nc.sync.dma_start(out=out_rows[P * m : P * (m + 1), cols], in_=result[:, 0:width])
 
         keep_busy(WARM_UP)
-        quantise_x(0, (4, 5), dummies=1)
-        quantise_x(1, (6, 7), dummies=1)
+        head = [(g, half) for g in range(2) for half in range(2)]
+        grouped_of = {}
+        for n, (g, half) in enumerate(head):
+            grouped_of[(g, half)] = flip(split_words(g, half), 4 + n, dummies=1)
+            if n >= 2:
+                quantise(grouped_of[head[n - 2]], head[n - 2][0], head[n - 2][1])
+        for g, half in head[2:]:
+            quantise(grouped_of[(g, half)], g, half)
 
         for j in range(N_CHUNKS - 1):
             first_bank = TOKEN_TILES * (j % 2)
@@ -190,7 +206,10 @@ def tile_virtual16bmatmul_kernel(
                 for m in range(TOKEN_TILES):
                     multiply(acc[m][:], chunk_cols[j], w, g, m, (w, g) == pieces[0], (w, g) == pieces[-1])
                 if j == 0 and w == n_weights - 1 and g + 2 < PASSES:
-                    quantise_x(g + 2, (4, 5) if g % 2 == 0 else (6, 7))
+                    halves = [split_words(g + 2, half) for half in range(2)]
+                    pair = [flip(halves[half], 4 + 2 * (g % 2) + half) for half in range(2)]
+                    for half in range(2):
+                        quantise(pair[half], g + 2, half)
             for m in range(TOKEN_TILES):
                 leave(acc[m][:], chunk_cols[j], m, m)
 

@@ -100,10 +100,11 @@ def tile_virtual16bmatmul_kernel(
             keep.tile([P, D_OUT], U8, name="w_planes_%d" % w, align_bytes=64)
             for w in range(n_weights)
         ]
+        w_landing = [keep.tile([P, D_OUT], U8, name="w_landing_%d" % w) for w in range(n_weights)]
 
         for j in range(N_CHUNKS):
             for w in range(n_weights):
-                nc.vector.memset(w_planes[w][:, chunk_cols[j]].bitcast(I32), 0)
+                nc.vector.memset(w_landing[w][:, chunk_cols[j]].bitcast(I32), 0)
 
         def load_x(g, first_tile, n_tiles):
             tiles = slice(first_tile, first_tile + n_tiles)
@@ -113,23 +114,30 @@ def tile_virtual16bmatmul_kernel(
             )
 
         load_x(0, 0, TILES_PER_BANK)
-        load_scale_planes(nc, w_planes[0], dram_scales[0], chunk_cols[0])
+        load_scale_planes(nc, w_landing[0], dram_scales[0], chunk_cols[0])
         load_x(0, TILES_PER_BANK, TILES_PER_BANK)
         load_x(1, 0, TILES_PER_BANK)
         load_x(1, TILES_PER_BANK, TILES_PER_BANK)
         load_words(nc, w_words[0], dram_words[0], 0, chunk_cols[0])
-        load_scale_planes(nc, w_planes[1], dram_scales[1], chunk_cols[0])
+        load_scale_planes(nc, w_landing[1], dram_scales[1], chunk_cols[0])
         load_words(nc, w_words[1], dram_words[1], 0, chunk_cols[0])
+        for g in range(2, PASSES):
+            load_x(g, 0, TOKEN_TILES)
         for g in range(1, PASSES):
-            if g + 1 < PASSES:
-                load_x(g + 1, 0, TOKEN_TILES)
             for w in range(n_weights):
                 load_words(nc, w_words[w], dram_words[w], g, chunk_cols[0])
         for j in range(1, N_CHUNKS):
             for w in range(n_weights):
-                load_scale_planes(nc, w_planes[w], dram_scales[w], chunk_cols[j])
+                load_scale_planes(nc, w_landing[w], dram_scales[w], chunk_cols[j])
                 for g in range(PASSES):
                     load_words(nc, w_words[w], dram_words[w], g, chunk_cols[j])
+
+        for j in range(N_CHUNKS):
+            for w in range(n_weights):
+                nc.gpsimd.tensor_copy(
+                    out=w_planes[w][:, chunk_cols[j]].bitcast(I32),
+                    in_=w_landing[w][:, chunk_cols[j]].bitcast(I32),
+                )
 
         def tiles_of(half):
             return slice(TILES_PER_BANK * half, TILES_PER_BANK * (half + 1))
@@ -205,11 +213,12 @@ def tile_virtual16bmatmul_kernel(
             for w, g in pieces:
                 for m in range(TOKEN_TILES):
                     multiply(acc[m][:], chunk_cols[j], w, g, m, (w, g) == pieces[0], (w, g) == pieces[-1])
-                if j == 0 and w == n_weights - 1 and g + 2 < PASSES:
-                    halves = [split_words(g + 2, half) for half in range(2)]
-                    pair = [flip(halves[half], 4 + 2 * (g % 2) + half) for half in range(2)]
-                    for half in range(2):
-                        quantise(pair[half], g + 2, half)
+                if j == 0 and (w, g) == (n_weights - 1, 0):
+                    rest = [(late, half) for late in range(2, PASSES) for half in range(2)]
+                    split_of = [split_words(late, half) for late, half in rest]
+                    ready = [flip(split_of[n], 4 + n) for n in range(len(rest))]
+                    for n, (late, half) in enumerate(rest):
+                        quantise(ready[n], late, half)
             for m in range(TOKEN_TILES):
                 leave(acc[m][:], chunk_cols[j], m, m)
 

@@ -20,8 +20,7 @@ PASSES = D_IN // K_PASS
 TOKEN_TILES = TOKENS // P
 N_COLS = 512
 N_CHUNKS = D_OUT // N_COLS
-WORDS_PER_PASS = K_PASS // 2
-TILES_PER_BANK = 2
+PAIR = 2
 QUADRANTS = 4
 PLANE_ROWS = 4
 PSUM_BANKS = 8
@@ -83,14 +82,17 @@ def tile_virtual16bmatmul_kernel(
             for i in range(n_matmuls):
                 nc.tensor.matmul(unread[:], lhsT=zeros[:, 0:P], rhs=zeros[:], start=True, stop=True)
 
-        x_raw = [keep.tile([P, TOKEN_TILES, K_PASS], BF16, name="x_raw_%d" % g) for g in range(PASSES)]
+        n_pairs = PASSES // PAIR
+        x_raw = [
+            keep.tile([P, TOKEN_TILES, PAIR * K_PASS], BF16, name="x_raw_%d" % b) for b in range(n_pairs)
+        ]
         x_codes = [
-            keep.tile([P, TOKEN_TILES, P], U32, name="x_codes_%d" % g, align_bytes=64)
-            for g in range(PASSES)
+            keep.tile([P, TOKEN_TILES, PAIR, P], U32, name="x_codes_%d" % b, align_bytes=64)
+            for b in range(n_pairs)
         ]
         x_scales = [
-            keep.tile([P, TOKEN_TILES, P], U8, name="x_scales_%d" % g, align_bytes=64)
-            for g in range(PASSES)
+            keep.tile([P, TOKEN_TILES, PAIR, P], U8, name="x_scales_%d" % b, align_bytes=64)
+            for b in range(n_pairs)
         ]
         w_words = [
             keep.tile([P, PASSES, D_OUT], U32, name="w_words_%d" % w, align_bytes=64)
@@ -106,23 +108,23 @@ def tile_virtual16bmatmul_kernel(
             for w in range(n_weights):
                 nc.vector.memset(w_landing[w][:, chunk_cols[j]].bitcast(I32), 0)
 
-        def load_x(g, first_tile, n_tiles):
+        def load_x(b, first_tile, n_tiles):
             tiles = slice(first_tile, first_tile + n_tiles)
+            width = PAIR * K_PASS
             nc.sync.dma_start(
-                out=x_raw[g][:, tiles, :],
-                in_=x_by_tile[:, tiles, K_PASS * g : K_PASS * (g + 1)],
+                out=x_raw[b][:, tiles, :],
+                in_=x_by_tile[:, tiles, width * b : width * (b + 1)],
             )
 
-        load_x(0, 0, TILES_PER_BANK)
+        load_x(0, 0, 1)
         load_scale_planes(nc, w_landing[0], dram_scales[0], chunk_cols[0])
-        load_x(0, TILES_PER_BANK, TILES_PER_BANK)
-        load_x(1, 0, TILES_PER_BANK)
-        load_x(1, TILES_PER_BANK, TILES_PER_BANK)
+        for m in range(1, TOKEN_TILES):
+            load_x(0, m, 1)
         load_words(nc, w_words[0], dram_words[0], 0, chunk_cols[0])
         load_scale_planes(nc, w_landing[1], dram_scales[1], chunk_cols[0])
         load_words(nc, w_words[1], dram_words[1], 0, chunk_cols[0])
-        for g in range(2, PASSES):
-            load_x(g, 0, TOKEN_TILES)
+        for half in range(2):
+            load_x(1, TOKEN_TILES // 2 * half, TOKEN_TILES // 2)
         for g in range(1, PASSES):
             for w in range(n_weights):
                 load_words(nc, w_words[w], dram_words[w], g, chunk_cols[0])
@@ -139,42 +141,39 @@ def tile_virtual16bmatmul_kernel(
                     in_=w_landing[w][:, chunk_cols[j]].bitcast(I32),
                 )
 
-        def tiles_of(half):
-            return slice(TILES_PER_BANK * half, TILES_PER_BANK * (half + 1))
-
-        def split_words(g, half):
-            x_split = stage.tile([P, TILES_PER_BANK, 2, P], F32, name="x_split")
+        def split_words(b, m):
+            x_split = stage.tile([P, PAIR, 2, P], F32, name="x_split")
             nc.vector.tensor_copy(
                 out=x_split[:],
-                in_=x_raw[g][:, tiles_of(half), :].bitcast(F32).rearrange("p i (r u) -> p i u r", u=2),
+                in_=x_raw[b][:, m, :].bitcast(F32).rearrange("p (i r u) -> p i u r", i=PAIR, u=2),
             )
             return x_split
 
         def flip(x_split, bank, dummies=0):
-            flipped = psum.tile([P, TILES_PER_BANK, 2, P], F32, name="flipped", tag="bank%d" % bank)
-            for i in range(TILES_PER_BANK):
+            flipped = psum.tile([P, PAIR, 2, P], F32, name="flipped", tag="bank%d" % bank)
+            for i in range(PAIR):
                 for u in range(2):
                     nc.tensor.transpose(flipped[:, i, u, :], x_split[:, i, u, :], identity[:])
             keep_busy(dummies)
-            grouped = stage.tile([P, TILES_PER_BANK, P, PACK], BF16, name="grouped", align_bytes=64)
+            grouped = stage.tile([P, PAIR, P, PACK], BF16, name="grouped", align_bytes=64)
             nc.scalar.copy(
                 out=grouped[:].bitcast(F32),
                 in_=flipped[:].rearrange("p i u r -> p i r u"),
             )
             return grouped
 
-        def quantise(grouped, g, half):
+        def quantise(grouped, b, m):
             nc.vector.quantize_mx(
-                out=x_codes[g][:, tiles_of(half), :].rearrange("p i r -> p (i r)").bitcast(FP8X4),
-                scales=x_scales[g][:, tiles_of(half), :].rearrange("p i r -> p (i r)"),
+                out=x_codes[b][:, m, :, :].rearrange("p i r -> p (i r)").bitcast(FP8X4),
+                scales=x_scales[b][:, m, :, :].rearrange("p i r -> p (i r)"),
                 in_=grouped[:].rearrange("p i r t -> p (i r t)"),
             )
 
         def multiply(group, cols, w, g, m, first, last):
             nc.tensor.matmul_mx(
                 out=group,
-                lhsT=x_codes[g][:, m, :].bitcast(FP8X4),
-                lhsT_scale=x_scales[g][:, m, :],
+                lhsT=x_codes[g // PAIR][:, m, g % PAIR, :].bitcast(FP8X4),
+                lhsT_scale=x_scales[g // PAIR][:, m, g % PAIR, :],
                 rhs=w_words[w][:, g, cols].bitcast(FP8X4),
                 rhs_scale=w_planes[w][PLANE_ROWS * g : P, cols],
                 start=first,
@@ -191,14 +190,13 @@ def tile_virtual16bmatmul_kernel(
             nc.sync.dma_start(out=out_rows[P * m : P * (m + 1), cols], in_=result[:, 0:width])
 
         keep_busy(WARM_UP)
-        head = [(g, half) for g in range(2) for half in range(2)]
-        grouped_of = {}
-        for n, (g, half) in enumerate(head):
-            grouped_of[(g, half)] = flip(split_words(g, half), 4 + n, dummies=1)
-            if n >= 2:
-                quantise(grouped_of[head[n - 2]], head[n - 2][0], head[n - 2][1])
-        for g, half in head[2:]:
-            quantise(grouped_of[(g, half)], g, half)
+        grouped_of = []
+        for m in range(TOKEN_TILES):
+            grouped_of.append(flip(split_words(0, m), TOKEN_TILES + m, dummies=1))
+            if m >= 2:
+                quantise(grouped_of[m - 2], 0, m - 2)
+        for m in range(2, TOKEN_TILES):
+            quantise(grouped_of[m], 0, m)
 
         for j in range(N_CHUNKS - 1):
             first_bank = TOKEN_TILES * (j % 2)
@@ -214,11 +212,10 @@ def tile_virtual16bmatmul_kernel(
                 for m in range(TOKEN_TILES):
                     multiply(acc[m][:], chunk_cols[j], w, g, m, (w, g) == pieces[0], (w, g) == pieces[-1])
                 if j == 0 and (w, g) == (n_weights - 1, 0):
-                    rest = [(late, half) for late in range(2, PASSES) for half in range(2)]
-                    split_of = [split_words(late, half) for late, half in rest]
-                    ready = [flip(split_of[n], 4 + n) for n in range(len(rest))]
-                    for n, (late, half) in enumerate(rest):
-                        quantise(ready[n], late, half)
+                    split_of = [split_words(1, tile) for tile in range(TOKEN_TILES)]
+                    ready = [flip(split_of[tile], TOKEN_TILES + tile) for tile in range(TOKEN_TILES)]
+                    for tile in range(TOKEN_TILES):
+                        quantise(ready[tile], 1, tile)
             for m in range(TOKEN_TILES):
                 leave(acc[m][:], chunk_cols[j], m, m)
 

@@ -30,9 +30,9 @@ WARM_UP = 5
 FLOPS = 2 * 2 * TOKENS * D_IN * D_OUT
 
 
-def load_scale_planes(nc, planes, scales, cols):
+def load_scale_planes(nc, planes, scales, cols, quadrants):
     rows = PASSES * PLANE_ROWS
-    for quadrant in range(QUADRANTS):
+    for quadrant in quadrants:
         nc.sync.dma_start(
             out=planes[32 * quadrant : 32 * quadrant + rows, cols].bitcast(I32),
             in_=scales[:, PLANE_ROWS * quadrant : PLANE_ROWS * (quadrant + 1), cols].bitcast(I32),
@@ -106,7 +106,7 @@ def tile_virtual16bmatmul_kernel(
 
         for j in range(N_CHUNKS):
             for w in range(n_weights):
-                nc.vector.memset(w_landing[w][:, chunk_cols[j]].bitcast(I32), 0)
+                nc.vector.memset(w_planes[w][:, chunk_cols[j]].bitcast(I32), 0)
 
         def load_x(b, first_tile, n_tiles):
             tiles = slice(first_tile, first_tile + n_tiles)
@@ -116,12 +116,13 @@ def tile_virtual16bmatmul_kernel(
                 in_=x_by_tile[:, tiles, width * b : width * (b + 1)],
             )
 
+        load_scale_planes(nc, w_landing[0], dram_scales[0], chunk_cols[0], range(1))
         load_x(0, 0, 1)
-        load_scale_planes(nc, w_landing[0], dram_scales[0], chunk_cols[0])
+        load_scale_planes(nc, w_landing[0], dram_scales[0], chunk_cols[0], range(1, QUADRANTS))
         for m in range(1, TOKEN_TILES):
             load_x(0, m, 1)
         load_words(nc, w_words[0], dram_words[0], 0, chunk_cols[0])
-        load_scale_planes(nc, w_landing[1], dram_scales[1], chunk_cols[0])
+        load_scale_planes(nc, w_landing[1], dram_scales[1], chunk_cols[0], range(QUADRANTS))
         load_words(nc, w_words[1], dram_words[1], 0, chunk_cols[0])
         for half in range(2):
             load_x(1, TOKEN_TILES // 2 * half, TOKEN_TILES // 2)
@@ -130,30 +131,35 @@ def tile_virtual16bmatmul_kernel(
                 load_words(nc, w_words[w], dram_words[w], g, chunk_cols[0])
         for j in range(1, N_CHUNKS):
             for w in range(n_weights):
-                load_scale_planes(nc, w_landing[w], dram_scales[w], chunk_cols[j])
+                load_scale_planes(nc, w_landing[w], dram_scales[w], chunk_cols[j], range(QUADRANTS))
                 for g in range(PASSES):
                     load_words(nc, w_words[w], dram_words[w], g, chunk_cols[j])
 
         for j in range(N_CHUNKS):
             for w in range(n_weights):
-                nc.gpsimd.tensor_copy(
-                    out=w_planes[w][:, chunk_cols[j]].bitcast(I32),
-                    in_=w_landing[w][:, chunk_cols[j]].bitcast(I32),
-                )
+                for quadrant in range(QUADRANTS):
+                    rows = slice(32 * quadrant, 32 * quadrant + PASSES * PLANE_ROWS)
+                    nc.gpsimd.tensor_copy(
+                        out=w_planes[w][rows, chunk_cols[j]].bitcast(I32),
+                        in_=w_landing[w][rows, chunk_cols[j]].bitcast(I32),
+                    )
+
+        def landed_words(b, m):
+            return x_raw[b][:, m, :].bitcast(F32).rearrange("p (i r u) -> p i u r", i=PAIR, u=2)
 
         def split_words(b, m):
             x_split = stage.tile([P, PAIR, 2, P], F32, name="x_split")
             nc.vector.tensor_copy(
                 out=x_split[:],
-                in_=x_raw[b][:, m, :].bitcast(F32).rearrange("p (i r u) -> p i u r", i=PAIR, u=2),
+                in_=landed_words(b, m),
             )
-            return x_split
+            return x_split[:]
 
         def flip(x_split, bank, dummies=0):
             flipped = psum.tile([P, PAIR, 2, P], F32, name="flipped", tag="bank%d" % bank)
             for i in range(PAIR):
                 for u in range(2):
-                    nc.tensor.transpose(flipped[:, i, u, :], x_split[:, i, u, :], identity[:])
+                    nc.tensor.transpose(flipped[:, i, u, :], x_split[:, i, u], identity[:])
             keep_busy(dummies)
             grouped = stage.tile([P, PAIR, P, PACK], BF16, name="grouped", align_bytes=64)
             nc.scalar.copy(
@@ -190,13 +196,31 @@ def tile_virtual16bmatmul_kernel(
             nc.sync.dma_start(out=out_rows[P * m : P * (m + 1), cols], in_=result[:, 0:width])
 
         keep_busy(WARM_UP)
+        last_tile = TOKEN_TILES - 1
         grouped_of = []
-        for m in range(TOKEN_TILES):
+        for m in range(last_tile):
             grouped_of.append(flip(split_words(0, m), TOKEN_TILES + m, dummies=1))
             if m >= 2:
                 quantise(grouped_of[m - 2], 0, m - 2)
-        for m in range(2, TOKEN_TILES):
+        halves = []
+        for i in range(PAIR):
+            flipped = psum.tile([P, 2, P], F32, name="flipped_half", tag="bank%d" % (PSUM_BANKS - 1 - 3 * i))
+            for u in range(2):
+                nc.tensor.transpose(flipped[:, u, :], landed_words(0, last_tile)[:, i, u], identity[:])
+            halves.append(flipped)
+        for m in range(last_tile - 2, last_tile):
             quantise(grouped_of[m], 0, m)
+        for i in range(PAIR):
+            grouped = stage.tile([P, P, PACK], BF16, name="grouped_half", align_bytes=64)
+            nc.scalar.copy(
+                out=grouped[:].bitcast(F32),
+                in_=halves[i][:].rearrange("p u r -> p r u"),
+            )
+            nc.vector.quantize_mx(
+                out=x_codes[0][:, last_tile, i, :].bitcast(FP8X4),
+                scales=x_scales[0][:, last_tile, i, :],
+                in_=grouped[:].rearrange("p r t -> p (r t)"),
+            )
 
         for j in range(N_CHUNKS - 1):
             first_bank = TOKEN_TILES * (j % 2)

@@ -71,9 +71,6 @@ def tile_virtual16bmatmul_kernel(
         results = ctx.enter_context(tc.tile_pool(name="results", bufs=8))
         psum = ctx.enter_context(tc.psum_pool(name="psum", bufs=1))
 
-        identity = keep.tile([P, P], F32, name="identity")
-        make_identity(nc, identity[:])
-
         zeros = keep.tile([P, N_COLS], BF16, name="zeros")
         nc.vector.memset(zeros[:], 0.0)
         unread = psum.tile([P, N_COLS], F32, name="unread", tag="bank0")
@@ -106,7 +103,11 @@ def tile_virtual16bmatmul_kernel(
 
         for j in range(N_CHUNKS):
             for w in range(n_weights):
-                nc.vector.memset(w_planes[w][:, chunk_cols[j]].bitcast(I32), 0)
+                engine = nc.gpsimd if (j, w) == (0, 0) else nc.vector
+                engine.memset(w_landing[w][:, chunk_cols[j]].bitcast(I32), 0)
+
+        identity = keep.tile([P, P], F32, name="identity")
+        make_identity(nc, identity[:])
 
         def load_x(b, first_tile, n_tiles):
             tiles = slice(first_tile, first_tile + n_tiles)
@@ -137,12 +138,10 @@ def tile_virtual16bmatmul_kernel(
 
         for j in range(N_CHUNKS):
             for w in range(n_weights):
-                for quadrant in range(QUADRANTS):
-                    rows = slice(32 * quadrant, 32 * quadrant + PASSES * PLANE_ROWS)
-                    nc.gpsimd.tensor_copy(
-                        out=w_planes[w][rows, chunk_cols[j]].bitcast(I32),
-                        in_=w_landing[w][rows, chunk_cols[j]].bitcast(I32),
-                    )
+                nc.gpsimd.tensor_copy(
+                    out=w_planes[w][:, chunk_cols[j]].bitcast(I32),
+                    in_=w_landing[w][:, chunk_cols[j]].bitcast(I32),
+                )
 
         def landed_words(b, m):
             return x_raw[b][:, m, :].bitcast(F32).rearrange("p (i r u) -> p i u r", i=PAIR, u=2)

from contextlib import ExitStack

import concourse.mybir as mybir
from concourse.masks import make_identity

F32 = mybir.dt.float32
BF16 = mybir.dt.bfloat16
I32 = mybir.dt.int32
U32 = mybir.dt.uint32
U8 = mybir.dt.uint8
FP8X4 = mybir.dt.float8_e4m3fn_x4

P = 128
PACK = 4
K_PASS = P * PACK
TOKENS = 512
D_IN = 2048
D_OUT = 2048
PASSES = D_IN // K_PASS
TOKEN_TILES = TOKENS // P
N_COLS = 512
N_CHUNKS = D_OUT // N_COLS
PAIR = 2
QUADRANTS = 4
PLANE_ROWS = 4
PSUM_BANKS = 8
LAST_WIDTHS = (256, 128, 128)
WARM_UP = 5

FLOPS = 2 * 2 * TOKENS * D_IN * D_OUT


def load_scale_planes(nc, planes, scales, cols, quadrants):
    rows = PASSES * PLANE_ROWS
    for quadrant in quadrants:
        nc.sync.dma_start(
            out=planes[32 * quadrant : 32 * quadrant + rows, cols].bitcast(I32),
            in_=scales[:, PLANE_ROWS * quadrant : PLANE_ROWS * (quadrant + 1), cols].bitcast(I32),
        )


def load_words(nc, words_sb, words, g, cols):
    nc.sync.dma_start(
        out=words_sb[:, g, cols].bitcast(I32),
        in_=words[g, :, cols, :].rearrange("p n t -> p (n t)").bitcast(I32),
    )


def tile_virtual16bmatmul_kernel(
    tc,
    x,
    weight_upper_words,
    weight_upper_scales,
    weight_lower_words,
    weight_lower_scales,
    out,
):
    nc = tc.nc
    x_rows = x.flatten_outer_dims()
    out_rows = out.flatten_outer_dims()
    x_by_tile = x_rows.rearrange("(m p) k -> p m k", p=P)
    dram_words = (weight_upper_words, weight_lower_words)
    dram_scales = (weight_upper_scales, weight_lower_scales)
    n_weights = len(dram_words)
    chunk_cols = [slice(N_COLS * j, N_COLS * (j + 1)) for j in range(N_CHUNKS)]

    with ExitStack() as ctx:
        ctx.enter_context(tc.manual_schedule())
        keep = ctx.enter_context(tc.tile_pool(name="keep", bufs=1))
        stage = ctx.enter_context(tc.tile_pool(name="stage", bufs=4))
        results = ctx.enter_context(tc.tile_pool(name="results", bufs=8))
        psum = ctx.enter_context(tc.psum_pool(name="psum", bufs=1))

        zeros = keep.tile([P, N_COLS], BF16, name="zeros")
        nc.vector.memset(zeros[:], 0.0)
        unread = psum.tile([P, N_COLS], F32, name="unread", tag="bank0")

        def keep_busy(n_matmuls):
            for i in range(n_matmuls):
                nc.tensor.matmul(unread[:], lhsT=zeros[:, 0:P], rhs=zeros[:], start=True, stop=True)

        n_pairs = PASSES // PAIR
        x_raw = [
            keep.tile([P, TOKEN_TILES, PAIR * K_PASS], BF16, name="x_raw_%d" % b) for b in range(n_pairs)
        ]
        x_codes = [
            keep.tile([P, TOKEN_TILES, PAIR, P], U32, name="x_codes_%d" % b, align_bytes=64)
            for b in range(n_pairs)
        ]
        x_scales = [
            keep.tile([P, TOKEN_TILES, PAIR, P], U8, name="x_scales_%d" % b, align_bytes=64)
            for b in range(n_pairs)
        ]
        w_words = [
            keep.tile([P, PASSES, D_OUT], U32, name="w_words_%d" % w, align_bytes=64)
            for w in range(n_weights)
        ]
        w_planes = [
            keep.tile([P, D_OUT], U8, name="w_planes_%d" % w, align_bytes=64)
            for w in range(n_weights)
        ]
        w_landing = [keep.tile([P, D_OUT], U8, name="w_landing_%d" % w) for w in range(n_weights)]

        for j in range(N_CHUNKS):
            for w in range(n_weights):
                engine = nc.gpsimd if (j, w) == (0, 0) else nc.vector
                engine.memset(w_landing[w][:, chunk_cols[j]].bitcast(I32), 0)

        identity = keep.tile([P, P], F32, name="identity")
        make_identity(nc, identity[:])

        def load_x(b, first_tile, n_tiles):
            tiles = slice(first_tile, first_tile + n_tiles)
            width = PAIR * K_PASS
            nc.sync.dma_start(
                out=x_raw[b][:, tiles, :],
                in_=x_by_tile[:, tiles, width * b : width * (b + 1)],
            )

        load_scale_planes(nc, w_landing[0], dram_scales[0], chunk_cols[0], range(1))
        load_x(0, 0, 1)
        load_scale_planes(nc, w_landing[0], dram_scales[0], chunk_cols[0], range(1, QUADRANTS))
        for m in range(1, TOKEN_TILES):
            load_x(0, m, 1)
        load_words(nc, w_words[0], dram_words[0], 0, chunk_cols[0])
        load_scale_planes(nc, w_landing[1], dram_scales[1], chunk_cols[0], range(QUADRANTS))
        load_words(nc, w_words[1], dram_words[1], 0, chunk_cols[0])
        for half in range(2):
            load_x(1, TOKEN_TILES // 2 * half, TOKEN_TILES // 2)
        for g in range(1, PASSES):
            for w in range(n_weights):
                load_words(nc, w_words[w], dram_words[w], g, chunk_cols[0])
        for j in range(1, N_CHUNKS):
            for w in range(n_weights):
                load_scale_planes(nc, w_landing[w], dram_scales[w], chunk_cols[j], range(QUADRANTS))
                for g in range(PASSES):
                    load_words(nc, w_words[w], dram_words[w], g, chunk_cols[j])

        for j in range(N_CHUNKS):
            for w in range(n_weights):
                nc.gpsimd.tensor_copy(
                    out=w_planes[w][:, chunk_cols[j]].bitcast(I32),
                    in_=w_landing[w][:, chunk_cols[j]].bitcast(I32),
                )

        def landed_words(b, m):
            return x_raw[b][:, m, :].bitcast(F32).rearrange("p (i r u) -> p i u r", i=PAIR, u=2)

        def split_words(b, m):
            x_split = stage.tile([P, PAIR, 2, P], F32, name="x_split")
            nc.vector.tensor_copy(
                out=x_split[:],
                in_=landed_words(b, m),
            )
            return x_split[:]

        def flip(x_split, bank, dummies=0):
            flipped = psum.tile([P, PAIR, 2, P], F32, name="flipped", tag="bank%d" % bank)
            for i in range(PAIR):
                for u in range(2):
                    nc.tensor.transpose(flipped[:, i, u, :], x_split[:, i, u], identity[:])
            keep_busy(dummies)
            grouped = stage.tile([P, PAIR, P, PACK], BF16, name="grouped", align_bytes=64)
            nc.scalar.copy(
                out=grouped[:].bitcast(F32),
                in_=flipped[:].rearrange("p i u r -> p i r u"),
            )
            return grouped

        def quantise(grouped, b, m):
            nc.vector.quantize_mx(
                out=x_codes[b][:, m, :, :].rearrange("p i r -> p (i r)").bitcast(FP8X4),
                scales=x_scales[b][:, m, :, :].rearrange("p i r -> p (i r)"),
                in_=grouped[:].rearrange("p i r t -> p (i r t)"),
            )

        def multiply(group, cols, w, g, m, first, last):
            nc.tensor.matmul_mx(
                out=group,
                lhsT=x_codes[g // PAIR][:, m, g % PAIR, :].bitcast(FP8X4),
                lhsT_scale=x_scales[g // PAIR][:, m, g % PAIR, :],
                rhs=w_words[w][:, g, cols].bitcast(FP8X4),
                rhs_scale=w_planes[w][PLANE_ROWS * g : P, cols],
                start=first,
                stop=last,
            )

        def leave(group, cols, m, turn):
            width = cols.stop - cols.start
            result = results.tile([P, N_COLS], F32, name="result")
            if turn % 2 == 0:
                nc.vector.tensor_copy(out=result[:, 0:width], in_=group)
            else:
                nc.scalar.copy(out=result[:, 0:width], in_=group)
            nc.sync.dma_start(out=out_rows[P * m : P * (m + 1), cols], in_=result[:, 0:width])

        keep_busy(WARM_UP)
        last_tile = TOKEN_TILES - 1
        grouped_of = []
        for m in range(last_tile):
            grouped_of.append(flip(split_words(0, m), TOKEN_TILES + m, dummies=1))
            if m >= 2:
                quantise(grouped_of[m - 2], 0, m - 2)
        halves = []
        for i in range(PAIR):
            flipped = psum.tile([P, 2, P], F32, name="flipped_half", tag="bank%d" % (PSUM_BANKS - 1 - 3 * i))
            for u in range(2):
                nc.tensor.transpose(flipped[:, u, :], landed_words(0, last_tile)[:, i, u], identity[:])
            halves.append(flipped)
        for m in range(last_tile - 2, last_tile):
            quantise(grouped_of[m], 0, m)
        for i in range(PAIR):
            grouped = stage.tile([P, P, PACK], BF16, name="grouped_half", align_bytes=64)
            nc.scalar.copy(
                out=grouped[:].bitcast(F32),
                in_=halves[i][:].rearrange("p u r -> p r u"),
            )
            nc.vector.quantize_mx(
                out=x_codes[0][:, last_tile, i, :].bitcast(FP8X4),
                scales=x_scales[0][:, last_tile, i, :],
                in_=grouped[:].rearrange("p r t -> p (r t)"),
            )

        for j in range(N_CHUNKS - 1):
            first_bank = TOKEN_TILES * (j % 2)
            acc = [
                psum.tile([P, N_COLS], F32, name="acc_%d" % m, tag="bank%d" % (first_bank + m))
                for m in range(TOKEN_TILES)
            ]
            if j == 0:
                pieces = [(w, g) for g in range(PASSES) for w in range(n_weights)]
            else:
                pieces = [(w, g) for w in range(n_weights) for g in range(PASSES)]
            for w, g in pieces:
                for m in range(TOKEN_TILES):
                    multiply(acc[m][:], chunk_cols[j], w, g, m, (w, g) == pieces[0], (w, g) == pieces[-1])
                if j == 0 and (w, g) == (n_weights - 1, 0):
                    split_of = [split_words(1, tile) for tile in range(TOKEN_TILES)]
                    ready = [flip(split_of[tile], TOKEN_TILES + tile) for tile in range(TOKEN_TILES)]
                    for tile in range(TOKEN_TILES):
                        quantise(ready[tile], 1, tile)
            for m in range(TOKEN_TILES):
                leave(acc[m][:], chunk_cols[j], m, m)

        first_col = N_COLS * (N_CHUNKS - 1)
        groups = [(m, first_col, N_COLS) for m in range(TOKEN_TILES - 1)]
        for width in LAST_WIDTHS:
            groups.append((TOKEN_TILES - 1, first_col, width))
            first_col += width
        pieces = [(w, g) for w in range(n_weights) for g in range(PASSES)]
        for turn, (m, col, width) in enumerate(groups):
            bank = (TOKEN_TILES + turn) % PSUM_BANKS
            acc_last = psum.tile([P, N_COLS], F32, name="acc_last", tag="bank%d" % bank)
            cols = slice(col, col + width)
            for w, g in pieces:
                multiply(acc_last[:, 0:width], cols, w, g, m, (w, g) == pieces[0], (w, g) == pieces[-1])
            leave(acc_last[:, 0:width], cols, m, turn)
